import numpy as np
import ml_dtypes


def mxq(x, axis, fmt="e4m3"):
    dtype, down = {"e4m3": (ml_dtypes.float8_e4m3fn, 7), "e5m2": (ml_dtypes.float8_e5m2, 14)}[fmt]
    v = np.moveaxis(np.asarray(x, np.float32).astype(ml_dtypes.bfloat16).astype(np.float64), axis, -1)
    blocks = v.reshape(v.shape[:-1] + (-1, 32))
    amax = np.abs(blocks).max(-1, keepdims=True)
    byte = np.maximum(np.where(amax > 0, np.frexp(amax)[1] - 1 + 127, 0) - down, 1)
    scale = np.exp2(byte - 127.0)
    codes = (blocks / scale).astype(np.float32).astype(dtype).astype(np.float64)
    return np.moveaxis((codes * scale).reshape(v.shape), -1, axis)


WIDE = False


def mx_kscale(k):
    if not WIDE:
        return np.ones(k)
    levels = np.array([10, -10, 5, -5, 0])
    if k % 512:
        return np.exp2(np.random.permutation(np.resize(levels, k // 32))).repeat(32)
    a = np.empty((k // 512, 16))
    for p in range(k // 512):
        a[p, :8] = np.random.permutation(np.resize(levels, 8))
        for g in range(8):
            far = levels[np.abs(levels - a[p, g]) >= 10]
            a[p, g + 8] = far[np.random.randint(len(far))]
    return np.exp2(a.ravel()).repeat(32)


BF16 = ml_dtypes.bfloat16


def bf(x):
    return np.asarray(x, np.float32).astype(BF16)


def f64(x):
    return np.asarray(x).astype(np.float64)


B, H, N, NMAX, NMIN, V, VI, NH = 4096, 1024, 127, 127, 126, 16, 3, 2
TS = 4.0


def distortion(X):
    cols = [np.sum(X[:, :-k] * X[:, k:], axis=1) for k in range(1, N + 1)]
    return np.stack(cols[::-1], axis=1)


def setup_inputs():
    s, t = mx_kscale(H), mx_kscale(H)
    return {"h1": bf(np.maximum(np.random.standard_normal((B, H)), 0.0) * s),
            "w_hid2": bf(np.random.standard_normal((H, H)) * 1.5 / np.sqrt(H) * t[:, None] / s[None, :]),
            "b_hid2": bf(np.random.standard_normal(H) * 0.2 * t),
            "w_out": bf(np.random.standard_normal((N + 1, H)) * 0.18 / np.sqrt(H) / t[None, :]),
            "b_out": bf(np.random.standard_normal(N + 1) * 0.03),
            "norm_root": bf(np.sqrt(TS * np.sqrt(N)) * np.exp(0.15 * np.random.standard_normal((B, 1)))),
            "T": bf(np.random.standard_normal((B, N)) * TS)}


def reference(h1, w_hid2, b_hid2, w_out, b_out, norm_root, T):
    h2 = np.maximum((mxq(f64(h1), 1, "e4m3") @ mxq(f64(w_hid2), 1, "e4m3").T) + f64(b_hid2), 0.0)
    X_hat = ((mxq(h2, 1, "e4m3") @ mxq(f64(w_out), 1, "e4m3").T) + f64(b_out)) * f64(norm_root)
    X_hat_clamped = np.clip(X_hat, -2.0, 2.0)
    error = np.reshape(np.mean((distortion(X_hat) - f64(T)) ** 2), (1,))
    error_clamped = np.reshape(np.mean((distortion(X_hat_clamped) - f64(T)) ** 2), (1,))
    return (X_hat, error, X_hat_clamped, error_clamped)

@@ -1,0 +1,414 @@
+from contextlib import ExitStack
+import math
+
+import concourse.masks as masks
+import concourse.mybir as mybir
+
+F32 = mybir.dt.float32
+BF16 = mybir.dt.bfloat16
+I32 = mybir.dt.int32
+U32 = mybir.dt.uint32
+U8 = mybir.dt.uint8
+FP8X4 = mybir.dt.float8_e4m3fn_x4
+ALU = mybir.AluOpType
+ACT = mybir.ActivationFunctionType
+AX = mybir.AxisListType
+
+P = 128
+B = 4096
+H = 1024
+NOUT = 128
+LAGS = 127
+G = 8
+TL = 4
+FLOPS = 2 * B * H * H + 2 * B * H * NOUT
+PIN = True
+RELU_ON_VECTOR = (3, 7)
+HEAD_U = 3
+TAIL_U = 2
+CLIP_T_ON_VECTOR = True
+GADD_ON_VECTOR = False
+
+
+def tile_qdtssolveronnx_pa_t_kernel(
+    tc, h1, w_hid2, b_hid2, w_out, b_out, norm_root, T, out_0, out_1, out_2, out_3
+):
+    nc = tc.nc
+    with ExitStack() as ctx:
+        if PIN:
+            ctx.enter_context(tc.manual_schedule())
+        const = ctx.enter_context(tc.tile_pool(name="const", bufs=1))
+        stage = ctx.enter_context(tc.tile_pool(name="stage", bufs=2))
+        psum = ctx.enter_context(tc.psum_pool(name="psum", bufs=8))
+
+        h1v = h1.rearrange("(g p t) k -> g p t k", g=G, p=P, t=TL)
+        wv = w_hid2.rearrange("(g p j) k -> g p j k", g=2, p=P, j=4)
+        tv = T.rearrange("(g p t) k -> p g (t k)", g=G, p=P, t=TL)
+        x_out = out_0.rearrange("(g p t) j -> g p t j", g=G, p=P, t=TL)
+        xc_out = out_2.rearrange("(g p t) j -> g p t j", g=G, p=P, t=TL)
+
+        hsb = {}
+
+        def load_h1(g):
+            t = stage.tile([P, TL, H], BF16, tag="hsb", bufs=3, name="hsb")
+            nc.sync.dma_start(out=t[:], in_=h1v[g])
+            hsb[g] = t
+
+        tsb = const.tile([P, G, 512], BF16, name="tsb")
+        nc.vector.memset(tsb[:, :, 496:512], 0.0)
+        for half in range(2):
+            nc.sync.dma_start(out=tsb[:, 4 * half : 4 * half + 4, 0 : TL * LAGS], in_=tv[:, 4 * half : 4 * half + 4, :])
+        load_h1(0)
+        wsb = []
+        for g2 in range(2):
+            wt = stage.tile([P, 4, H], BF16, tag="sq", bufs=2, name="wsb")
+            wsb.append(wt)
+            for h in range(2):
+                nc.sync.dma_start(out=wt[:, 2 * h : 2 * h + 2, :], in_=wv[g2][:, 2 * h : 2 * h + 2, :])
+        wosb = const.tile([P, H], BF16, name="wosb")
+        nc.scalar.dma_start(out=wosb[:], in_=w_out)
+        bh_b = const.tile([P, 2, 4], BF16, name="bh_b")
+        bo_b = const.tile([P, 1], BF16, name="bo_b")
+        with nc.allow_non_contiguous_dma(reason="two small bias vectors, one or four elements a partition"):
+            nc.scalar.dma_start(out=bh_b[:], in_=b_hid2.rearrange("(g p j) -> p g j", g=2, p=P, j=4))
+            nc.scalar.dma_start(out=bo_b[:], in_=b_out.rearrange("(p o) -> p o", o=1))
+        load_h1(1)
+        nb = const.tile([P, B], BF16, name="nb")
+        nc.sync.dma_start(out=nb[:], in_=norm_root.rearrange("b o -> (b o)").partition_broadcast(P))
+        load_h1(2)
+
+        odd_i = const.tile([P, P], I32, name="odd_i")
+        nc.gpsimd.iota(odd_i[:], pattern=[[2, P]], base=1, channel_multiplier=0)
+        row_i = const.tile([P, 1], I32, name="row_i")
+        nc.gpsimd.iota(row_i[:], pattern=[[1, 1]], base=0, channel_multiplier=1)
+        ident_b = const.tile([P, P], BF16, name="ident_b")
+        masks.make_identity(nc, ident_b[:])
+        ident_f = const.tile([P, P], F32, name="ident_f")
+        masks.make_identity(nc, ident_f[:])
+
+        odd_f = const.tile([P, P], F32, name="odd_f")
+        nc.vector.tensor_copy(out=odd_f[:], in_=odd_i[:])
+        row_f = const.tile([P, 1], F32, name="row_f")
+        nc.vector.tensor_copy(out=row_f[:], in_=row_i[:])
+        lag_f = const.tile([P, 1], F32, name="lag_f")
+        nc.vector.tensor_scalar(out=lag_f[:], in0=row_f[:], scalar1=-1.0, scalar2=float(LAGS), op0=ALU.mult, op1=ALU.add)
+        lag_w = const.tile([P, 1], F32, name="lag_w")
+        nc.vector.tensor_scalar(out=lag_w[:], in0=row_f[:], scalar1=float(LAGS), scalar2=2.0, op0=ALU.is_lt, op1=ALU.mult)
+        cnt_f = const.tile([P, 3, P], F32, name="cnt_f")
+        nc.vector.tensor_scalar(out=cnt_f[:, 0, :], in0=odd_f[:], scalar1=row_f[:, 0:1], scalar2=384.0, op0=ALU.mult, op1=ALU.add)
+        nc.vector.tensor_scalar(out=cnt_f[:, 1, :], in0=odd_f[:], scalar1=row_f[:, 0:1], scalar2=256.0, op0=ALU.mult, op1=ALU.add)
+        nc.vector.tensor_scalar(out=cnt_f[:, 2, :], in0=odd_f[:], scalar1=lag_f[:, 0:1], scalar2=384.0, op0=ALU.mult, op1=ALU.add)
+        cnt_i = const.tile([P, 3, P], I32, name="cnt_i")
+        nc.vector.tensor_copy(out=cnt_i[:], in_=cnt_f[:])
+        cnt_m = const.tile([P, 3, P], I32, name="cnt_m")
+        nc.vector.tensor_single_scalar(out=cnt_m[:], in_=cnt_i[:], scalar=511, op=ALU.bitwise_and)
+        ang = const.tile([P, 3, P], F32, name="ang")
+        nc.vector.tensor_copy(out=ang[:], in_=cnt_m[:])
+        nc.vector.tensor_scalar(out=ang[:], in0=ang[:], scalar1=-256.0, scalar2=math.pi / 256.0, op0=ALU.add, op1=ALU.mult)
+        trig = const.tile([P, 3, P], F32, name="trig")
+        nc.scalar.activation(out=trig[:], in_=ang[:], func=ACT.Sin)
+        ftab = trig[:, 0:2, :].rearrange("p a m -> p (a m)")
+        ctab = const.tile([P, P], F32, name="ctab")
+        nc.vector.tensor_scalar(out=ctab[:], in0=trig[:, 2, :], scalar1=lag_w[:, 0:1], scalar2=None, op0=ALU.mult)
+
+        bh = const.tile([P, 8], F32, name="bh")
+        nc.vector.tensor_copy(out=bh[:], in_=bh_b[:].rearrange("p g j -> p (g j)"))
+        bo = const.tile([P, 1], F32, name="bo")
+        nc.vector.tensor_copy(out=bo[:], in_=bo_b[:])
+        fin = const.tile([P, P], F32, name="fin")
+        nc.vector.memset(fin[:], 0.0)
+
+        count = float(B * LAGS)
+        r0acc = const.tile([P, 2, G * TL], F32, name="r0acc")
+        s1 = const.tile([P, 2, G + 1], F32, name="s1")
+
+        def copy_out(which, out, in_):
+            if which == 0:
+                nc.vector.tensor_copy(out=out, in_=in_)
+            else:
+                nc.scalar.copy(out=out, in_=in_)
+
+        def word_transposes(words):
+            pt = psum.tile([P, 2, 2, P], F32, tag="bank", name="pt")
+            for gk in range(2):
+                for u in range(2):
+                    nc.tensor.transpose(pt[:, gk, u, :], words(gk, u), ident_f[:])
+            return pt
+
+        tta = const.tile([P, G, TL, P], F32, name="tta")
+        usb = const.tile([P, G, TL * P], F32, name="usb")
+
+        def transpose_t(g):
+            ptt = psum.tile([P, TL, P], BF16, tag="bank", name="ptt")
+            for tl in range(TL):
+                nc.tensor.transpose(ptt[:, tl, :], tsb[:, g, LAGS * tl : LAGS * tl + P], ident_b[:])
+            copy_out(g % 2, tta[:, g], ptt[:])
+
+        def transform_t(g):
+            pu = psum.tile([P, TL, P], F32, tag="bank", name="pu")
+            for tl in range(TL):
+                nc.tensor.matmul(pu[:, tl, :], lhsT=tta[:, g, tl, :], rhs=ctab[:], start=True, stop=True)
+            copy_out(1 - g % 2, usb[:, g, :], pu[:].rearrange("p t m -> p (t m)"))
+
+        hg = {}
+        hq = {}
+        hs = {}
+
+        def transpose_h1(g):
+            hw = hsb[g][:].bitcast(F32)
+            grouped = stage.tile([P, 2, TL, P, 4], BF16, tag="hg", bufs=2, name="hg", align_bytes=64)
+            gw = grouped[:].bitcast(F32)
+            for tl in range(TL):
+                pt = word_transposes(lambda gk, u: hw[:, tl, 256 * gk + u : 256 * (gk + 1) : 2])
+                copy_out(tl % 2, gw[:, :, tl, :, :], pt[:].rearrange("p g u c -> p g c u"))
+            hg[g] = grouped
+
+        def quantise_h1(g):
+            codes = stage.tile([P, 2 * 512], U32, tag="hq", bufs=2, name="hq", align_bytes=64)
+            scales = stage.tile([P, 2 * 512], U8, tag="hs", bufs=2, name="hs", align_bytes=64)
+            nc.vector.quantize_mx(
+                out=codes[:].bitcast(FP8X4), scales=scales[:], in_=hg[g][:].rearrange("p g t c f -> p (g t c f)")
+            )
+            hq[g] = codes
+            hs[g] = scales
+
+        wq = const.tile([P, 8, 2, P], U32, name="wq", align_bytes=64)
+        ws = const.tile([P, 8, 2, P], U8, name="ws", align_bytes=64)
+        woq = const.tile([P, 2, P], U32, name="woq", align_bytes=64)
+        wos = const.tile([P, 2, P], U8, name="wos", align_bytes=64)
+
+        def prepare_w(pair):
+            grouped = stage.tile([P, 2, 2, P, 4], BF16, tag="wg", bufs=2, name="wg", align_bytes=64)
+            gw = grouped[:].bitcast(F32)
+            for h in range(2):
+                ht = 2 * pair + h
+                ww = wsb[ht // 4][:].bitcast(F32)
+                pt = word_transposes(lambda gk, u: ww[:, ht % 4, 256 * gk + u : 256 * (gk + 1) : 2])
+                copy_out(h, gw[:, h], pt[:].rearrange("p g u c -> p g c u"))
+            return grouped
+
+        def quantise_w(pair, grouped):
+            nc.vector.quantize_mx(
+                out=wq[:, 2 * pair : 2 * pair + 2].rearrange("p h g c -> p (h g c)").bitcast(FP8X4),
+                scales=ws[:, 2 * pair : 2 * pair + 2].rearrange("p h g c -> p (h g c)"),
+                in_=grouped[:].rearrange("p h g c f -> p (h g c f)"),
+            )
+
+        def prepare_w_out():
+            wow = wosb[:].bitcast(F32).rearrange("o (g p u) -> o g u p", g=2, p=P, u=2)
+            grouped = stage.tile([P, 2, P, 4], BF16, tag="wog", bufs=1, name="wog", align_bytes=64)
+            pt = word_transposes(lambda g2, u: wow[:, g2, u, :])
+            copy_out(1, grouped[:].bitcast(F32), pt[:].rearrange("p g u c -> p g c u"))
+            return grouped
+
+        def quantise_w_out(grouped):
+            nc.vector.quantize_mx(
+                out=woq[:].rearrange("p g c -> p (g c)").bitcast(FP8X4),
+                scales=wos[:].rearrange("p g c -> p (g c)"),
+                in_=grouped[:].rearrange("p g c f -> p (g c f)"),
+            )
+
+        h2q = {}
+        h2s = {}
+        planes = {}
+
+        def layer1(g, ht):
+            if ht == 0:
+                h2q[g] = stage.tile([P, 2, 512], U32, tag="h2q", bufs=2, name="h2q", align_bytes=64)
+                h2s[g] = stage.tile([P, 2, 512], U8, tag="h2s", bufs=2, name="h2s", align_bytes=64)
+            if ht % 4 == 0:
+                planes[g] = stage.tile([P, 4, 512], BF16, tag="h2p", bufs=3, name="h2p")
+            pm = psum.tile([P, 512], F32, tag="bank", name="pm")
+            for gk in range(2):
+                nc.tensor.matmul_mx(
+                    out=pm[:],
+                    lhsT=wq[:, ht, gk, :].bitcast(FP8X4),
+                    lhsT_scale=ws[:, ht, gk, :],
+                    rhs=hq[g][:, 512 * gk : 512 * gk + 512].bitcast(FP8X4),
+                    rhs_scale=hs[g][:, 512 * gk : 512 * gk + 512],
+                    start=(gk == 0),
+                    stop=(gk == 1),
+                )
+            if ht in RELU_ON_VECTOR:
+                nc.vector.tensor_scalar(
+                    out=planes[g][:, ht % 4, :], in0=pm[:], scalar1=bh[:, ht : ht + 1], scalar2=0.0, op0=ALU.add, op1=ALU.max
+                )
+            else:
+                nc.scalar.activation(out=planes[g][:, ht % 4, :], in_=pm[:], func=ACT.Relu, bias=bh[:, ht : ht + 1])
+
+        def regroup_h2(g):
+            grouped = stage.tile([P, 512, 4], BF16, tag="h2g", bufs=2, name="h2g", align_bytes=64)
+            nc.vector.tensor_copy(
+                out=grouped[:].rearrange("p (c i) t -> p c t i", i=4),
+                in_=planes[g][:].rearrange("p t (c i) -> p c t i", i=4),
+            )
+            return grouped
+
+        def quantise_h2(g, g2, grouped):
+            nc.vector.quantize_mx(
+                out=h2q[g][:, g2, :].bitcast(FP8X4), scales=h2s[g][:, g2, :], in_=grouped[:].rearrange("p c t -> p (c t)")
+            )
+
+        nbv = nb[:].rearrange("p (g c t) -> p g t c", g=G, c=P, t=TL)
+        xt = {}
+        xct = {}
+        sq = {}
+        gt = {}
+        dt_ = {}
+
+        def layer2(g):
+            pm = psum.tile([P, 512], F32, tag="bank", name="pm2")
+            for g2 in range(2):
+                nc.tensor.matmul_mx(
+                    out=pm[:],
+                    lhsT=woq[:, g2, :].bitcast(FP8X4),
+                    lhsT_scale=wos[:, g2, :],
+                    rhs=h2q[g][:, g2, :].bitcast(FP8X4),
+                    rhs_scale=h2s[g][:, g2, :],
+                    start=(g2 == 0),
+                    stop=(g2 == 1),
+                )
+            xt[g] = stage.tile([P, TL, P], F32, tag="xt", bufs=2, name="xt")
+            nc.vector.scalar_tensor_tensor(
+                out=xt[g][:],
+                in0=pm[:].rearrange("p (t c) -> p t c", t=TL),
+                scalar=bo[:, 0:1],
+                in1=nbv[:, g],
+                op0=ALU.add,
+                op1=ALU.mult,
+            )
+            xct[g] = stage.tile([P, TL, P], F32, tag="xct", bufs=2, name="xct")
+            eng = nc.vector if CLIP_T_ON_VECTOR else nc.gpsimd
+            eng.tensor_scalar(out=xct[g][:], in0=xt[g][:], scalar1=2.0, scalar2=-2.0, op0=ALU.min, op1=ALU.max)
+
+        def natural_x(g):
+            px = psum.tile([P, TL, P], F32, tag="bank", name="px")
+            for tl in range(TL):
+                nc.tensor.transpose(px[:, tl, :], xt[g][:, tl, :], ident_f[:])
+            xn = stage.tile([P, TL, P], F32, tag="xn", bufs=2, name="xn")
+            nc.scalar.copy(out=xn[:], in_=px[:])
+            xcn = stage.tile([P, TL, P], F32, tag="xcn", bufs=2, name="xcn")
+            nc.gpsimd.tensor_scalar(out=xcn[:], in0=xn[:], scalar1=2.0, scalar2=-2.0, op0=ALU.min, op1=ALU.max)
+            nc.sync.dma_start(out=x_out[g], in_=xn[:])
+            nc.sync.dma_start(out=xc_out[g], in_=xcn[:])
+
+        def spectrum(g, tl, add_on_vector):
+            if tl == 0:
+                sq[g] = stage.tile([P, TL, 2, 2 * P], F32, tag="sq", bufs=2, name="sq")
+                gt[g] = stage.tile([P, 2, TL, P], F32, tag="gt", bufs=2, name="gt")
+            pd = psum.tile([P, 2, 2 * P], F32, tag="bank", name="pd")
+            nc.tensor.matmul(pd[:, 0, :], lhsT=xt[g][:, tl, :], rhs=ftab, start=True, stop=True)
+            nc.tensor.matmul(pd[:, 1, :], lhsT=xct[g][:, tl, :], rhs=ftab, start=True, stop=True)
+            for y in range(2):
+                nc.scalar.activation(
+                    out=sq[g][:, tl, y, :],
+                    in_=pd[:, y, :],
+                    func=ACT.Square,
+                    accum_out=r0acc[:, y, TL * g + tl : TL * g + tl + 1],
+                )
+            if tl % 2 == 1:
+                eng = nc.vector if add_on_vector else nc.gpsimd
+                eng.tensor_tensor(
+                    out=gt[g][:, :, tl - 1 : tl + 1, :],
+                    in0=sq[g][:, tl - 1 : tl + 1, :, 0:P].rearrange("p t y m -> p y t m"),
+                    in1=sq[g][:, tl - 1 : tl + 1, :, P : 2 * P].rearrange("p t y m -> p y t m"),
+                    op=ALU.add,
+                )
+
+        def difference(g, t0, nt):
+            if t0 == 0:
+                dt_[g] = stage.tile([P, 2, TL, P], F32, tag="dt", bufs=2, name="dt")
+            nc.vector.tensor_tensor(
+                out=dt_[g][:, :, t0 : t0 + nt, :].rearrange("p y t m -> p y (t m)"),
+                in0=gt[g][:, :, t0 : t0 + nt, :].rearrange("p y t m -> p y (t m)"),
+                in1=usb[:, g, P * t0 : P * (t0 + nt)].unsqueeze(1).to_broadcast([P, 2, P * nt]),
+                op=ALU.subtract,
+            )
+
+        def sum_squares(g, y, t0, nt, col):
+            junk = stage.tile([P, TL * P], F32, tag="junk", bufs=1, name="junk")
+            nc.scalar.activation(
+                out=junk[:, 0 : P * nt],
+                in_=dt_[g][:, y, t0 : t0 + nt, :].rearrange("p t m -> p (t m)"),
+                func=ACT.Square,
+                scale=(1.0 / (256.0 * count)) ** 0.5,
+                accum_out=s1[:, y, col : col + 1],
+            )
+
+        for g in range(G):
+            transpose_t(g)
+        transform_t(0)
+        transform_t(1)
+        transpose_h1(0)
+        transform_t(2)
+        wg0 = prepare_w(0)
+        quantise_h1(0)
+        wg1 = prepare_w(1)
+        quantise_w(0, wg0)
+        wg2 = prepare_w(2)
+        quantise_w(1, wg1)
+        wg3 = prepare_w(3)
+        quantise_w(2, wg2)
+        wog = prepare_w_out()
+        quantise_w(3, wg3)
+        quantise_w_out(wog)
+
+        for i in range(G + 1):
+            if i + 3 < G:
+                load_h1(i + 3)
+            if i + 1 < G:
+                transpose_h1(i + 1)
+            if i >= 2:
+                natural_x(i - 2)
+            if i >= 1:
+                layer2(i - 1)
+            if 2 <= i < G:
+                difference(i - 2, 0, TL)
+            if i < G:
+                for ht in range(4):
+                    layer1(i, ht)
+                ga = regroup_h2(i)
+                for ht in range(4, 8):
+                    layer1(i, ht)
+                quantise_h2(i, 0, ga)
+                gb = regroup_h2(i)
+                if i + 1 < G:
+                    quantise_h1(i + 1)
+                quantise_h2(i, 1, gb)
+            if i == 0:
+                for g in range(HEAD_U, G - TAIL_U):
+                    transform_t(g)
+            if 1 <= i < G:
+                for tl in range(TL):
+                    spectrum(i - 1, tl, GADD_ON_VECTOR)
+                    if i >= 2 and tl < 2:
+                        sum_squares(i - 2, tl, 0, TL, i - 2)
+            if i == G:
+                for g in range(G - TAIL_U, G):
+                    transform_t(g)
+                natural_x(G - 1)
+                difference(G - 2, 0, TL)
+                for tl in range(TL):
+                    spectrum(G - 1, tl, True)
+                    if tl < 2:
+                        sum_squares(G - 2, tl, 0, TL, G - 2)
+                    if tl % 2 == 1:
+                        difference(G - 1, tl - 1, 2)
+                        for y in range(2):
+                            sum_squares(G - 1, y, tl - 1, 2, G - 1 + tl // 2)
+
+        s2 = const.tile([P, 2], F32, name="s2")
+        for y in range(2):
+            junk2 = const.tile([P, G * TL], F32, name="junk2")
+            nc.scalar.activation(out=junk2[:], in_=r0acc[:, y, :], func=ACT.Square, accum_out=s2[:, y : y + 1])
+        s1t = const.tile([P, 2], F32, name="s1t")
+        nc.vector.tensor_reduce(out=s1t[:], in_=s1[:], axis=AX.X, op=ALU.add)
+        nc.vector.scalar_tensor_tensor(
+            out=fin[:, 0:2], in0=s2[:], scalar=-1.0 / (2.0 * 128.0 * 128.0 * count), in1=s1t[:], op0=ALU.mult, op1=ALU.add
+        )
+        pf = psum.tile([P, P], F32, tag="bank", name="pf")
+        nc.tensor.transpose(pf[:], fin[:], ident_f[:])
+        res = const.tile([P, 1], F32, name="res")
+        nc.vector.tensor_reduce(out=res[:], in_=pf[:], axis=AX.X, op=ALU.add)
+        nc.sync.dma_start(out=out_1.rearrange("(a b) -> a b", a=1), in_=res[0:1, 0:1])
+        nc.scalar.dma_start(out=out_3.rearrange("(a b) -> a b", a=1), in_=res[1:2, 0:1])

@@ -22,12 +22,7 @@ LAGS = 127
 G = 8
 TL = 4
 FLOPS = 2 * B * H * H + 2 * B * H * NOUT
-PIN = True
 RELU_ON_VECTOR = (3, 7)
-HEAD_U = 3
-TAIL_U = 2
-CLIP_T_ON_VECTOR = True
-GADD_ON_VECTOR = False
 
 
 def tile_qdtssolveronnx_pa_t_kernel(
@@ -35,8 +30,7 @@ def tile_qdtssolveronnx_pa_t_kernel(
 ):
     nc = tc.nc
     with ExitStack() as ctx:
-        if PIN:
-            ctx.enter_context(tc.manual_schedule())
+        ctx.enter_context(tc.manual_schedule())
         const = ctx.enter_context(tc.tile_pool(name="const", bufs=1))
         stage = ctx.enter_context(tc.tile_pool(name="stage", bufs=2))
         psum = ctx.enter_context(tc.psum_pool(name="psum", bufs=8))
@@ -56,8 +50,8 @@ def tile_qdtssolveronnx_pa_t_kernel(
 
         tsb = const.tile([P, G, 512], BF16, name="tsb")
         nc.vector.memset(tsb[:, :, 496:512], 0.0)
-        for half in range(2):
-            nc.sync.dma_start(out=tsb[:, 4 * half : 4 * half + 4, 0 : TL * LAGS], in_=tv[:, 4 * half : 4 * half + 4, :])
+        for g0, g1 in ((0, 2), (2, 5), (5, G)):
+            nc.sync.dma_start(out=tsb[:, g0:g1, 0 : TL * LAGS], in_=tv[:, g0:g1, :])
         load_h1(0)
         wsb = []
         for g2 in range(2):
@@ -110,17 +104,26 @@ def tile_qdtssolveronnx_pa_t_kernel(
         ftab = trig[:, 0:2, :].rearrange("p a m -> p (a m)")
         ctab = const.tile([P, P], F32, name="ctab")
         nc.vector.tensor_scalar(out=ctab[:], in0=trig[:, 2, :], scalar1=lag_w[:, 0:1], scalar2=None, op0=ALU.mult)
+        cterm = const.tile([P, 3, P], BF16, name="cterm")
+        crest = const.tile([P, 2, P], F32, name="crest")
+        nc.vector.tensor_copy(out=cterm[:, 0, :], in_=ctab[:])
+        nc.vector.tensor_tensor(out=crest[:, 0, :], in0=ctab[:], in1=cterm[:, 0, :], op=ALU.subtract)
+        nc.vector.tensor_copy(out=cterm[:, 1, :], in_=crest[:, 0, :])
+        nc.vector.tensor_tensor(out=crest[:, 1, :], in0=crest[:, 0, :], in1=cterm[:, 1, :], op=ALU.subtract)
+        nc.vector.tensor_copy(out=cterm[:, 2, :], in_=crest[:, 1, :])
 
         bh = const.tile([P, 8], F32, name="bh")
         nc.vector.tensor_copy(out=bh[:], in_=bh_b[:].rearrange("p g j -> p (g j)"))
         bo = const.tile([P, 1], F32, name="bo")
         nc.vector.tensor_copy(out=bo[:], in_=bo_b[:])
-        fin = const.tile([P, P], F32, name="fin")
-        nc.vector.memset(fin[:], 0.0)
 
         count = float(B * LAGS)
         r0acc = const.tile([P, 2, G * TL], F32, name="r0acc")
-        s1 = const.tile([P, 2, G + 1], F32, name="s1")
+        s1 = const.tile([P, G + 4, 2], F32, name="s1")
+        ones = const.tile([P, P], F32, name="ones")
+        nc.gpsimd.memset(ones[:], 1.0)
+        minus = const.tile([P, P], F32, name="minus")
+        nc.gpsimd.memset(minus[:], -1.0)
 
         def copy_out(which, out, in_):
             if which == 0:
@@ -135,7 +138,7 @@ def tile_qdtssolveronnx_pa_t_kernel(
                     nc.tensor.transpose(pt[:, gk, u, :], words(gk, u), ident_f[:])
             return pt
 
-        tta = const.tile([P, G, TL, P], F32, name="tta")
+        tta = const.tile([P, G, TL, P], BF16, name="tta")
         usb = const.tile([P, G, TL * P], F32, name="usb")
 
         def transpose_t(g):
@@ -144,23 +147,33 @@ def tile_qdtssolveronnx_pa_t_kernel(
                 nc.tensor.transpose(ptt[:, tl, :], tsb[:, g, LAGS * tl : LAGS * tl + P], ident_b[:])
             copy_out(g % 2, tta[:, g], ptt[:])
 
-        def transform_t(g):
+        def transform_t(g, which):
             pu = psum.tile([P, TL, P], F32, tag="bank", name="pu")
             for tl in range(TL):
-                nc.tensor.matmul(pu[:, tl, :], lhsT=tta[:, g, tl, :], rhs=ctab[:], start=True, stop=True)
-            copy_out(1 - g % 2, usb[:, g, :], pu[:].rearrange("p t m -> p (t m)"))
+                for term in range(3):
+                    nc.tensor.matmul(
+                        pu[:, tl, :], lhsT=tta[:, g, tl, :], rhs=cterm[:, term, :], start=(term == 0), stop=(term == 2)
+                    )
+            copy_out(which, usb[:, g, :], pu[:].rearrange("p t m -> p (t m)"))
 
         hg = {}
         hq = {}
         hs = {}
 
-        def transpose_h1(g):
-            hw = hsb[g][:].bitcast(F32)
+        hp = {}
+
+        def permute_h1(g):
+            hp[g] = stage.tile([P, TL * 2, 2, P], F32, tag="hp", bufs=2, name="hp")
+            nc.vector.tensor_copy(
+                out=hp[g][:], in_=hsb[g][:].bitcast(F32).rearrange("p t (g c u) -> p (t g) u c", g=2, u=2)
+            )
+
+        def transpose_h1(g, engines):
             grouped = stage.tile([P, 2, TL, P, 4], BF16, tag="hg", bufs=2, name="hg", align_bytes=64)
             gw = grouped[:].bitcast(F32)
             for tl in range(TL):
-                pt = word_transposes(lambda gk, u: hw[:, tl, 256 * gk + u : 256 * (gk + 1) : 2])
-                copy_out(tl % 2, gw[:, :, tl, :, :], pt[:].rearrange("p g u c -> p g c u"))
+                pt = word_transposes(lambda gk, u: hp[g][:, 2 * tl + gk, u, :])
+                copy_out(engines[tl % 2], gw[:, :, tl, :, :], pt[:].rearrange("p g u c -> p g c u"))
             hg[g] = grouped
 
         def quantise_h1(g):
@@ -184,7 +197,7 @@ def tile_qdtssolveronnx_pa_t_kernel(
                 ht = 2 * pair + h
                 ww = wsb[ht // 4][:].bitcast(F32)
                 pt = word_transposes(lambda gk, u: ww[:, ht % 4, 256 * gk + u : 256 * (gk + 1) : 2])
-                copy_out(h, gw[:, h], pt[:].rearrange("p g u c -> p g c u"))
+                copy_out(1, gw[:, h], pt[:].rearrange("p g u c -> p g c u"))
             return grouped
 
         def quantise_w(pair, grouped):
@@ -278,21 +291,20 @@ def tile_qdtssolveronnx_pa_t_kernel(
                 op1=ALU.mult,
             )
             xct[g] = stage.tile([P, TL, P], F32, tag="xct", bufs=2, name="xct")
-            eng = nc.vector if CLIP_T_ON_VECTOR else nc.gpsimd
-            eng.tensor_scalar(out=xct[g][:], in0=xt[g][:], scalar1=2.0, scalar2=-2.0, op0=ALU.min, op1=ALU.max)
+            nc.vector.tensor_scalar(out=xct[g][:], in0=xt[g][:], scalar1=2.0, scalar2=-2.0, op0=ALU.min, op1=ALU.max)
 
-        def natural_x(g):
+        def natural_x(g, which):
             px = psum.tile([P, TL, P], F32, tag="bank", name="px")
             for tl in range(TL):
                 nc.tensor.transpose(px[:, tl, :], xt[g][:, tl, :], ident_f[:])
             xn = stage.tile([P, TL, P], F32, tag="xn", bufs=2, name="xn")
-            nc.scalar.copy(out=xn[:], in_=px[:])
+            copy_out(which, xn[:], px[:])
             xcn = stage.tile([P, TL, P], F32, tag="xcn", bufs=2, name="xcn")
             nc.gpsimd.tensor_scalar(out=xcn[:], in0=xn[:], scalar1=2.0, scalar2=-2.0, op0=ALU.min, op1=ALU.max)
             nc.sync.dma_start(out=x_out[g], in_=xn[:])
             nc.sync.dma_start(out=xc_out[g], in_=xcn[:])
 
-        def spectrum(g, tl, add_on_vector):
+        def spectrum(g, tl):
             if tl == 0:
                 sq[g] = stage.tile([P, TL, 2, 2 * P], F32, tag="sq", bufs=2, name="sq")
                 gt[g] = stage.tile([P, 2, TL, P], F32, tag="gt", bufs=2, name="gt")
@@ -306,14 +318,14 @@ def tile_qdtssolveronnx_pa_t_kernel(
                     func=ACT.Square,
                     accum_out=r0acc[:, y, TL * g + tl : TL * g + tl + 1],
                 )
-            if tl % 2 == 1:
-                eng = nc.vector if add_on_vector else nc.gpsimd
-                eng.tensor_tensor(
-                    out=gt[g][:, :, tl - 1 : tl + 1, :],
-                    in0=sq[g][:, tl - 1 : tl + 1, :, 0:P].rearrange("p t y m -> p y t m"),
-                    in1=sq[g][:, tl - 1 : tl + 1, :, P : 2 * P].rearrange("p t y m -> p y t m"),
-                    op=ALU.add,
-                )
+
+        def power(g, t0, nt, eng):
+            eng.tensor_tensor(
+                out=gt[g][:, :, t0 : t0 + nt, :],
+                in0=sq[g][:, t0 : t0 + nt, :, 0:P].rearrange("p t y m -> p y t m"),
+                in1=sq[g][:, t0 : t0 + nt, :, P : 2 * P].rearrange("p t y m -> p y t m"),
+                op=ALU.add,
+            )
 
         def difference(g, t0, nt):
             if t0 == 0:
@@ -332,21 +344,49 @@ def tile_qdtssolveronnx_pa_t_kernel(
                 in_=dt_[g][:, y, t0 : t0 + nt, :].rearrange("p t m -> p (t m)"),
                 func=ACT.Square,
                 scale=(1.0 / (256.0 * count)) ** 0.5,
-                accum_out=s1[:, y, col : col + 1],
+                accum_out=s1[:, col, y : y + 1],
             )
+
+        def sum_squares_v(g, y, t0, nt, col):
+            junk = stage.tile([P, TL * P], F32, tag="junkv", bufs=1, name="junkv")
+            d = dt_[g][:, y, t0 : t0 + nt, :].rearrange("p t m -> p (t m)")
+            nc.vector.scalar_tensor_tensor(
+                out=junk[:, 0 : P * nt],
+                in0=d,
+                scalar=1.0 / (256.0 * count),
+                in1=d,
+                op0=ALU.mult,
+                op1=ALU.mult,
+                accum_out=s1[:, col, y : y + 1],
+            )
+
+        def sum_r0(t0, t1, col):
+            for y in range(2):
+                junk = stage.tile([P, G * TL], F32, tag="junkr", bufs=1, name="junkr")
+                nc.scalar.activation(
+                    out=junk[:, 0 : t1 - t0],
+                    in_=r0acc[:, y, t0:t1],
+                    func=ACT.Square,
+                    scale=(1.0 / (2.0 * 128.0 * 128.0 * count)) ** 0.5,
+                    accum_out=s1[:, col, y : y + 1],
+                )
 
         for g in range(G):
             transpose_t(g)
-        transform_t(0)
-        transform_t(1)
-        transpose_h1(0)
-        transform_t(2)
+        transform_t(0, 1)
+        transform_t(1, 1)
+        permute_h1(0)
+        transpose_h1(0, (0, 1))
+        transform_t(2, 1)
         wg0 = prepare_w(0)
+        transform_t(3, 1)
         quantise_h1(0)
         wg1 = prepare_w(1)
         quantise_w(0, wg0)
+        transform_t(4, 1)
         wg2 = prepare_w(2)
         quantise_w(1, wg1)
+        permute_h1(1)
         wg3 = prepare_w(3)
         quantise_w(2, wg2)
         wog = prepare_w_out()
@@ -357,9 +397,11 @@ def tile_qdtssolveronnx_pa_t_kernel(
             if i + 3 < G:
                 load_h1(i + 3)
             if i + 1 < G:
-                transpose_h1(i + 1)
+                transpose_h1(i + 1, (0, 1))
+            if i + 2 < G:
+                permute_h1(i + 2)
             if i >= 2:
-                natural_x(i - 2)
+                natural_x(i - 2, 1)
             if i >= 1:
                 layer2(i - 1)
             if 2 <= i < G:
@@ -376,39 +418,51 @@ def tile_qdtssolveronnx_pa_t_kernel(
                     quantise_h1(i + 1)
                 quantise_h2(i, 1, gb)
             if i == 0:
-                for g in range(HEAD_U, G - TAIL_U):
-                    transform_t(g)
+                for g in range(5, G):
+                    transform_t(g, 1)
             if 1 <= i < G:
                 for tl in range(TL):
-                    spectrum(i - 1, tl, GADD_ON_VECTOR)
+                    spectrum(i - 1, tl)
+                    if tl % 2 == 1:
+                        power(i - 1, tl - 1, 2, nc.gpsimd)
                     if i >= 2 and tl < 2:
                         sum_squares(i - 2, tl, 0, TL, i - 2)
             if i == G:
-                for g in range(G - TAIL_U, G):
-                    transform_t(g)
-                natural_x(G - 1)
                 difference(G - 2, 0, TL)
                 for tl in range(TL):
-                    spectrum(G - 1, tl, True)
-                    if tl < 2:
-                        sum_squares(G - 2, tl, 0, TL, G - 2)
-                    if tl % 2 == 1:
-                        difference(G - 1, tl - 1, 2)
-                        for y in range(2):
-                            sum_squares(G - 1, y, tl - 1, 2, G - 1 + tl // 2)
+                    spectrum(G - 1, tl)
+                    if tl == 0:
+                        sum_r0(0, TL * (G - 1), G + 2)
+                    else:
+                        t0, nt = (0, 2) if tl == 1 else (tl, 1)
+                        power(G - 1, t0, nt, nc.vector)
+                        difference(G - 1, t0, nt)
+                        sum_squares_v(G - 1, 0, t0, nt, G - 2 + tl)
+                        if tl < 3:
+                            sum_squares(G - 2, tl - 1, 0, TL, G - 2)
+                            sum_squares_v(G - 1, 1, t0, nt, G - 2 + tl)
+                        else:
+                            sum_r0(TL * (G - 1), TL * G, G + 3)
+                            sum_squares(G - 1, 1, t0, nt, G - 2 + tl)
+                    if tl == 1:
+                        natural_x(G - 1, 0)
 
-        s2 = const.tile([P, 2], F32, name="s2")
-        for y in range(2):
-            junk2 = const.tile([P, G * TL], F32, name="junk2")
-            nc.scalar.activation(out=junk2[:], in_=r0acc[:, y, :], func=ACT.Square, accum_out=s2[:, y : y + 1])
-        s1t = const.tile([P, 2], F32, name="s1t")
-        nc.vector.tensor_reduce(out=s1t[:], in_=s1[:], axis=AX.X, op=ALU.add)
-        nc.vector.scalar_tensor_tensor(
-            out=fin[:, 0:2], in0=s2[:], scalar=-1.0 / (2.0 * 128.0 * 128.0 * count), in1=s1t[:], op0=ALU.mult, op1=ALU.add
+        pf = psum.tile([P, G + 4, 2], F32, tag="bank", name="pf")
+        nc.tensor.matmul(
+            pf[:, G + 2 :, :].rearrange("p c y -> p (c y)"),
+            lhsT=minus[:],
+            rhs=s1[:, G + 2 :, :].rearrange("p c y -> p (c y)"),
+            start=True,
+            stop=True,
         )
-        pf = psum.tile([P, P], F32, tag="bank", name="pf")
-        nc.tensor.transpose(pf[:], fin[:], ident_f[:])
-        res = const.tile([P, 1], F32, name="res")
-        nc.vector.tensor_reduce(out=res[:], in_=pf[:], axis=AX.X, op=ALU.add)
+        nc.tensor.matmul(
+            pf[:, 0 : G + 2, :].rearrange("p c y -> p (c y)"),
+            lhsT=ones[:],
+            rhs=s1[:, 0 : G + 2, :].rearrange("p c y -> p (c y)"),
+            start=True,
+            stop=True,
+        )
+        res = const.tile([P, 2], F32, name="res")
+        nc.vector.tensor_reduce(out=res[:], in_=pf[:].rearrange("p c y -> p y c"), axis=AX.X, op=ALU.add)
         nc.sync.dma_start(out=out_1.rearrange("(a b) -> a b", a=1), in_=res[0:1, 0:1])
-        nc.scalar.dma_start(out=out_3.rearrange("(a b) -> a b", a=1), in_=res[1:2, 0:1])
+        nc.scalar.dma_start(out=out_3.rearrange("(a b) -> a b", a=1), in_=res[0:1, 1:2])

@@ -397,7 +397,7 @@ def tile_qdtssolveronnx_pa_t_kernel(
             if i + 3 < G:
                 load_h1(i + 3)
             if i + 1 < G:
-                transpose_h1(i + 1, (0, 1))
+                transpose_h1(i + 1, (1, 1))
             if i + 2 < G:
                 permute_h1(i + 2)
             if i >= 2:
@@ -424,7 +424,7 @@ def tile_qdtssolveronnx_pa_t_kernel(
                 for tl in range(TL):
                     spectrum(i - 1, tl)
                     if tl % 2 == 1:
-                        power(i - 1, tl - 1, 2, nc.gpsimd)
+                        power(i - 1, tl - 1, 2, nc.vector)
                     if i >= 2 and tl < 2:
                         sum_squares(i - 2, tl, 0, TL, i - 2)
             if i == G:

@@ -190,13 +190,21 @@ def tile_qdtssolveronnx_pa_t_kernel(
         woq = const.tile([P, 2, P], U32, name="woq", align_bytes=64)
         wos = const.tile([P, 2, P], U8, name="wos", align_bytes=64)
 
+        wp = {}
+
+        def permute_w(pair):
+            wp[pair] = stage.tile([P, 4, 2, P], F32, tag="wp", bufs=3, name="wp")
+            rows = 2 * (pair % 2)
+            nc.vector.tensor_copy(
+                out=wp[pair][:],
+                in_=wsb[pair // 2][:, rows : rows + 2, :].bitcast(F32).rearrange("p t (g c u) -> p (t g) u c", g=2, u=2),
+            )
+
         def prepare_w(pair):
             grouped = stage.tile([P, 2, 2, P, 4], BF16, tag="wg", bufs=2, name="wg", align_bytes=64)
             gw = grouped[:].bitcast(F32)
             for h in range(2):
-                ht = 2 * pair + h
-                ww = wsb[ht // 4][:].bitcast(F32)
-                pt = word_transposes(lambda gk, u: ww[:, ht % 4, 256 * gk + u : 256 * (gk + 1) : 2])
+                pt = word_transposes(lambda gk, u: wp[pair][:, 2 * h + gk, u, :])
                 copy_out(1, gw[:, h], pt[:].rearrange("p g u c -> p g c u"))
             return grouped
 
@@ -376,14 +384,18 @@ def tile_qdtssolveronnx_pa_t_kernel(
         transform_t(0, 1)
         transform_t(1, 1)
         permute_h1(0)
+        permute_w(0)
         transpose_h1(0, (0, 1))
         transform_t(2, 1)
+        permute_w(1)
         wg0 = prepare_w(0)
         transform_t(3, 1)
         quantise_h1(0)
+        permute_w(2)
         wg1 = prepare_w(1)
         quantise_w(0, wg0)
         transform_t(4, 1)
+        permute_w(3)
         wg2 = prepare_w(2)
         quantise_w(1, wg1)
         permute_h1(1)
@@ -396,15 +408,18 @@ def tile_qdtssolveronnx_pa_t_kernel(
         for i in range(G + 1):
             if i + 3 < G:
                 load_h1(i + 3)
-            if i + 1 < G:
+            if i < 2:
                 transpose_h1(i + 1, (1, 1))
-            if i + 2 < G:
                 permute_h1(i + 2)
-            if i >= 2:
-                natural_x(i - 2, 1)
+            if i == G:
+                power(G - 2, 2, 2, nc.gpsimd)
+                difference(G - 2, 0, 2)
             if i >= 1:
                 layer2(i - 1)
+            if i == G:
+                natural_x(G - 2, 1)
             if 2 <= i < G:
+                power(i - 2, 2, 2, nc.vector)
                 difference(i - 2, 0, TL)
             if i < G:
                 for ht in range(4):
@@ -423,29 +438,38 @@ def tile_qdtssolveronnx_pa_t_kernel(
             if 1 <= i < G:
                 for tl in range(TL):
                     spectrum(i - 1, tl)
-                    if tl % 2 == 1:
-                        power(i - 1, tl - 1, 2, nc.vector)
+                    if tl == 1:
+                        power(i - 1, 0, 2, nc.vector)
+                    if tl == 1:
+                        if i + 2 < G:
+                            transpose_h1(i + 2, (1, 1))
+                        if i + 3 < G:
+                            permute_h1(i + 3)
+                        if i < G - 1:
+                            natural_x(i - 1, 1)
                     if i >= 2 and tl < 2:
                         sum_squares(i - 2, tl, 0, TL, i - 2)
             if i == G:
-                difference(G - 2, 0, TL)
+                difference(G - 2, 2, 2)
+                sum_r0(0, TL * (G - 1), G + 2)
+                sum_squares_v(G - 2, 0, 0, TL, G - 2)
                 for tl in range(TL):
                     spectrum(G - 1, tl)
-                    if tl == 0:
-                        sum_r0(0, TL * (G - 1), G + 2)
-                    else:
+                    if tl == 1:
+                        sum_squares(G - 2, 1, 0, TL, G - 2)
+                    if tl >= 1:
                         t0, nt = (0, 2) if tl == 1 else (tl, 1)
                         power(G - 1, t0, nt, nc.vector)
                         difference(G - 1, t0, nt)
-                        sum_squares_v(G - 1, 0, t0, nt, G - 2 + tl)
-                        if tl < 3:
-                            sum_squares(G - 2, tl - 1, 0, TL, G - 2)
-                            sum_squares_v(G - 1, 1, t0, nt, G - 2 + tl)
-                        else:
-                            sum_r0(TL * (G - 1), TL * G, G + 3)
-                            sum_squares(G - 1, 1, t0, nt, G - 2 + tl)
-                    if tl == 1:
-                        natural_x(G - 1, 0)
+                        if tl == 1:
+                            for y in range(2):
+                                sum_squares_v(G - 1, y, t0, nt, G - 2 + tl)
+                sum_r0(TL * (G - 1), TL * G, G + 3)
+                natural_x(G - 1, 1)
+                sum_squares_v(G - 1, 0, 3, 1, G + 1)
+                for y in range(2):
+                    sum_squares(G - 1, y, 2, 1, G)
+                sum_squares(G - 1, 1, 3, 1, G + 1)
 
         pf = psum.tile([P, G + 4, 2], F32, tag="bank", name="pf")
         nc.tensor.matmul(

@@ -50,7 +50,7 @@ def tile_qdtssolveronnx_pa_t_kernel(
 
         tsb = const.tile([P, G, 512], BF16, name="tsb")
         nc.vector.memset(tsb[:, :, 496:512], 0.0)
-        for g0, g1 in ((0, 2), (2, 5), (5, G)):
+        for g0, g1 in ((0, 1), (1, 4), (4, G)):
             nc.sync.dma_start(out=tsb[:, g0:g1, 0 : TL * LAGS], in_=tv[:, g0:g1, :])
         load_h1(0)
         wsb = []
@@ -298,16 +298,18 @@ def tile_qdtssolveronnx_pa_t_kernel(
                 op0=ALU.add,
                 op1=ALU.mult,
             )
+
+        def clip_x(g):
             xct[g] = stage.tile([P, TL, P], F32, tag="xct", bufs=2, name="xct")
             nc.vector.tensor_scalar(out=xct[g][:], in0=xt[g][:], scalar1=2.0, scalar2=-2.0, op0=ALU.min, op1=ALU.max)
 
-        def natural_x(g, which):
+        def natural_x(g):
             px = psum.tile([P, TL, P], F32, tag="bank", name="px")
             for tl in range(TL):
                 nc.tensor.transpose(px[:, tl, :], xt[g][:, tl, :], ident_f[:])
             xn = stage.tile([P, TL, P], F32, tag="xn", bufs=2, name="xn")
-            copy_out(which, xn[:], px[:])
             xcn = stage.tile([P, TL, P], F32, tag="xcn", bufs=2, name="xcn")
+            nc.scalar.copy(out=xn[:], in_=px[:])
             nc.gpsimd.tensor_scalar(out=xcn[:], in0=xn[:], scalar1=2.0, scalar2=-2.0, op0=ALU.min, op1=ALU.max)
             nc.sync.dma_start(out=x_out[g], in_=xn[:])
             nc.sync.dma_start(out=xc_out[g], in_=xcn[:])
@@ -408,23 +410,29 @@ def tile_qdtssolveronnx_pa_t_kernel(
         for i in range(G + 1):
             if i + 3 < G:
                 load_h1(i + 3)
-            if i < 2:
-                transpose_h1(i + 1, (1, 1))
-                permute_h1(i + 2)
+            if i == 1:
+                transpose_h1(2, (1, 1))
+                permute_h1(3)
             if i == G:
                 power(G - 2, 2, 2, nc.gpsimd)
                 difference(G - 2, 0, 2)
             if i >= 1:
                 layer2(i - 1)
-            if i == G:
-                natural_x(G - 2, 1)
             if 2 <= i < G:
                 power(i - 2, 2, 2, nc.vector)
+            if i >= 1:
+                clip_x(i - 1)
+            if i == G:
+                natural_x(G - 2)
+            if 2 <= i < G:
                 difference(i - 2, 0, TL)
             if i < G:
                 for ht in range(4):
                     layer1(i, ht)
                 ga = regroup_h2(i)
+                if i == 0:
+                    transpose_h1(1, (1, 1))
+                    permute_h1(2)
                 for ht in range(4, 8):
                     layer1(i, ht)
                 quantise_h2(i, 0, ga)
@@ -446,7 +454,7 @@ def tile_qdtssolveronnx_pa_t_kernel(
                         if i + 3 < G:
                             permute_h1(i + 3)
                         if i < G - 1:
-                            natural_x(i - 1, 1)
+                            natural_x(i - 1)
                     if i >= 2 and tl < 2:
                         sum_squares(i - 2, tl, 0, TL, i - 2)
             if i == G:
@@ -461,14 +469,14 @@ def tile_qdtssolveronnx_pa_t_kernel(
                         t0, nt = (0, 2) if tl == 1 else (tl, 1)
                         power(G - 1, t0, nt, nc.vector)
                         difference(G - 1, t0, nt)
-                        if tl == 1:
-                            for y in range(2):
-                                sum_squares_v(G - 1, y, t0, nt, G - 2 + tl)
-                sum_r0(TL * (G - 1), TL * G, G + 3)
-                natural_x(G - 1, 1)
+                    if tl == 2:
+                        sum_squares_v(G - 1, 0, 0, 2, G - 1)
+                natural_x(G - 1)
                 sum_squares_v(G - 1, 0, 3, 1, G + 1)
+                sum_squares(G - 1, 1, 0, 2, G - 1)
                 for y in range(2):
                     sum_squares(G - 1, y, 2, 1, G)
+                sum_r0(TL * (G - 1), TL * G, G + 3)
                 sum_squares(G - 1, 1, 3, 1, G + 1)
 
         pf = psum.tile([P, G + 4, 2], F32, tag="bank", name="pf")

@@ -41,6 +41,12 @@ def tile_qdtssolveronnx_pa_t_kernel(
         x_out = out_0.rearrange("(g p t) j -> g p t j", g=G, p=P, t=TL)
         xc_out = out_2.rearrange("(g p t) j -> g p t j", g=G, p=P, t=TL)
 
+        ones = const.tile([P, P], F32, name="ones")
+        nc.vector.memset(ones[:], 1.0)
+        warm = psum.tile([P, 512], F32, tag="bank", name="warm")
+        for n in range(4):
+            nc.tensor.matmul(warm[:, 0:P], lhsT=ones[:], rhs=ones[:], start=True, stop=True)
+
         hsb = {}
 
         def load_h1(g):
@@ -71,57 +77,45 @@ def tile_qdtssolveronnx_pa_t_kernel(
         nc.sync.dma_start(out=nb[:], in_=norm_root.rearrange("b o -> (b o)").partition_broadcast(P))
         load_h1(2)
 
-        odd_i = const.tile([P, P], I32, name="odd_i")
-        nc.gpsimd.iota(odd_i[:], pattern=[[2, P]], base=1, channel_multiplier=0)
-        row_i = const.tile([P, 1], I32, name="row_i")
-        nc.gpsimd.iota(row_i[:], pattern=[[1, 1]], base=0, channel_multiplier=1)
+        odd_f = const.tile([P, P], F32, name="odd_f")
+        nc.gpsimd.iota(odd_f[:], pattern=[[2, P]], base=1, channel_multiplier=0, allow_small_or_imprecise_dtypes=True)
+        row_f = const.tile([P, 1], F32, name="row_f")
+        nc.gpsimd.iota(row_f[:], pattern=[[1, 1]], base=0, channel_multiplier=1, allow_small_or_imprecise_dtypes=True)
         ident_b = const.tile([P, P], BF16, name="ident_b")
         masks.make_identity(nc, ident_b[:])
         ident_f = const.tile([P, P], F32, name="ident_f")
         masks.make_identity(nc, ident_f[:])
 
-        odd_f = const.tile([P, P], F32, name="odd_f")
-        nc.vector.tensor_copy(out=odd_f[:], in_=odd_i[:])
-        row_f = const.tile([P, 1], F32, name="row_f")
-        nc.vector.tensor_copy(out=row_f[:], in_=row_i[:])
         lag_f = const.tile([P, 1], F32, name="lag_f")
         nc.vector.tensor_scalar(out=lag_f[:], in0=row_f[:], scalar1=-1.0, scalar2=float(LAGS), op0=ALU.mult, op1=ALU.add)
         lag_w = const.tile([P, 1], F32, name="lag_w")
         nc.vector.tensor_scalar(out=lag_w[:], in0=row_f[:], scalar1=float(LAGS), scalar2=2.0, op0=ALU.is_lt, op1=ALU.mult)
-        cnt_f = const.tile([P, 3, P], F32, name="cnt_f")
-        nc.vector.tensor_scalar(out=cnt_f[:, 0, :], in0=odd_f[:], scalar1=row_f[:, 0:1], scalar2=384.0, op0=ALU.mult, op1=ALU.add)
-        nc.vector.tensor_scalar(out=cnt_f[:, 1, :], in0=odd_f[:], scalar1=row_f[:, 0:1], scalar2=256.0, op0=ALU.mult, op1=ALU.add)
-        nc.vector.tensor_scalar(out=cnt_f[:, 2, :], in0=odd_f[:], scalar1=lag_f[:, 0:1], scalar2=384.0, op0=ALU.mult, op1=ALU.add)
         cnt_i = const.tile([P, 3, P], I32, name="cnt_i")
-        nc.vector.tensor_copy(out=cnt_i[:], in_=cnt_f[:])
+        nc.vector.tensor_scalar(out=cnt_i[:, 2, :], in0=odd_f[:], scalar1=lag_f[:, 0:1], scalar2=384.0, op0=ALU.mult, op1=ALU.add)
+        nc.vector.tensor_scalar(out=cnt_i[:, 0, :], in0=odd_f[:], scalar1=row_f[:, 0:1], scalar2=384.0, op0=ALU.mult, op1=ALU.add)
+        nc.vector.tensor_scalar(out=cnt_i[:, 1, :], in0=odd_f[:], scalar1=row_f[:, 0:1], scalar2=256.0, op0=ALU.mult, op1=ALU.add)
         cnt_m = const.tile([P, 3, P], I32, name="cnt_m")
         nc.vector.tensor_single_scalar(out=cnt_m[:], in_=cnt_i[:], scalar=511, op=ALU.bitwise_and)
         ang = const.tile([P, 3, P], F32, name="ang")
-        nc.vector.tensor_copy(out=ang[:], in_=cnt_m[:])
-        nc.vector.tensor_scalar(out=ang[:], in0=ang[:], scalar1=-256.0, scalar2=math.pi / 256.0, op0=ALU.add, op1=ALU.mult)
+        nc.vector.tensor_scalar(out=ang[:], in0=cnt_m[:], scalar1=-256.0, scalar2=math.pi / 256.0, op0=ALU.add, op1=ALU.mult)
         trig = const.tile([P, 3, P], F32, name="trig")
         nc.scalar.activation(out=trig[:], in_=ang[:], func=ACT.Sin)
         ftab = trig[:, 0:2, :].rearrange("p a m -> p (a m)")
-        ctab = const.tile([P, P], F32, name="ctab")
-        nc.vector.tensor_scalar(out=ctab[:], in0=trig[:, 2, :], scalar1=lag_w[:, 0:1], scalar2=None, op0=ALU.mult)
         cterm = const.tile([P, 3, P], BF16, name="cterm")
-        crest = const.tile([P, 2, P], F32, name="crest")
-        nc.vector.tensor_copy(out=cterm[:, 0, :], in_=ctab[:])
-        nc.vector.tensor_tensor(out=crest[:, 0, :], in0=ctab[:], in1=cterm[:, 0, :], op=ALU.subtract)
-        nc.vector.tensor_copy(out=cterm[:, 1, :], in_=crest[:, 0, :])
-        nc.vector.tensor_tensor(out=crest[:, 1, :], in0=crest[:, 0, :], in1=cterm[:, 1, :], op=ALU.subtract)
-        nc.vector.tensor_copy(out=cterm[:, 2, :], in_=crest[:, 1, :])
+        crest = const.tile([P, P], F32, name="crest")
+        nc.vector.tensor_scalar(out=cterm[:, 0, :], in0=trig[:, 2, :], scalar1=lag_w[:, 0:1], scalar2=None, op0=ALU.mult)
+        nc.vector.scalar_tensor_tensor(
+            out=crest[:], in0=trig[:, 2, :], scalar=lag_w[:, 0:1], in1=cterm[:, 0, :], op0=ALU.mult, op1=ALU.subtract
+        )
+        nc.vector.tensor_copy(out=cterm[:, 1, :], in_=crest[:])
+        nc.vector.tensor_tensor(out=cterm[:, 2, :], in0=crest[:], in1=cterm[:, 1, :], op=ALU.subtract)
 
         bh = const.tile([P, 8], F32, name="bh")
-        nc.vector.tensor_copy(out=bh[:], in_=bh_b[:].rearrange("p g j -> p (g j)"))
         bo = const.tile([P, 1], F32, name="bo")
-        nc.vector.tensor_copy(out=bo[:], in_=bo_b[:])
 
         count = float(B * LAGS)
         r0acc = const.tile([P, 2, G * TL], F32, name="r0acc")
         s1 = const.tile([P, G + 4, 2], F32, name="s1")
-        ones = const.tile([P, P], F32, name="ones")
-        nc.gpsimd.memset(ones[:], 1.0)
         minus = const.tile([P, P], F32, name="minus")
         nc.gpsimd.memset(minus[:], -1.0)
 
@@ -393,6 +387,8 @@ def tile_qdtssolveronnx_pa_t_kernel(
         wg0 = prepare_w(0)
         transform_t(3, 1)
         quantise_h1(0)
+        nc.vector.tensor_copy(out=bh[:], in_=bh_b[:].rearrange("p g j -> p (g j)"))
+        nc.vector.tensor_copy(out=bo[:], in_=bo_b[:])
         permute_w(2)
         wg1 = prepare_w(1)
         quantise_w(0, wg0)
@@ -435,14 +431,17 @@ def tile_qdtssolveronnx_pa_t_kernel(
                     permute_h1(2)
                 for ht in range(4, 8):
                     layer1(i, ht)
-                quantise_h2(i, 0, ga)
                 gb = regroup_h2(i)
+                quantise_h2(i, 0, ga)
+                quantise_h2(i, 1, gb)
                 if i + 1 < G:
                     quantise_h1(i + 1)
-                quantise_h2(i, 1, gb)
             if i == 0:
                 for g in range(5, G):
                     transform_t(g, 1)
+            if 2 <= i < G:
+                for y in range(2):
+                    sum_squares(i - 2, y, 0, TL, i - 2)
             if 1 <= i < G:
                 for tl in range(TL):
                     spectrum(i - 1, tl)
@@ -455,8 +454,6 @@ def tile_qdtssolveronnx_pa_t_kernel(
                             permute_h1(i + 3)
                         if i < G - 1:
                             natural_x(i - 1)
-                    if i >= 2 and tl < 2:
-                        sum_squares(i - 2, tl, 0, TL, i - 2)
             if i == G:
                 difference(G - 2, 2, 2)
                 sum_r0(0, TL * (G - 1), G + 2)

@@ -73,9 +73,10 @@ def tile_qdtssolveronnx_pa_t_kernel(
             nc.scalar.dma_start(out=bh_b[:], in_=b_hid2.rearrange("(g p j) -> p g j", g=2, p=P, j=4))
             nc.scalar.dma_start(out=bo_b[:], in_=b_out.rearrange("(p o) -> p o", o=1))
         load_h1(1)
+        load_h1(2)
         nb = const.tile([P, B], BF16, name="nb")
         nc.sync.dma_start(out=nb[:], in_=norm_root.rearrange("b o -> (b o)").partition_broadcast(P))
-        load_h1(2)
+        load_h1(3)
 
         odd_f = const.tile([P, P], F32, name="odd_f")
         nc.gpsimd.iota(odd_f[:], pattern=[[2, P]], base=1, channel_multiplier=0, allow_small_or_imprecise_dtypes=True)
@@ -404,22 +405,21 @@ def tile_qdtssolveronnx_pa_t_kernel(
         quantise_w_out(wog)
 
         for i in range(G + 1):
-            if i + 3 < G:
-                load_h1(i + 3)
+            if i + 4 < G:
+                load_h1(i + 4)
             if i == 1:
                 transpose_h1(2, (1, 1))
                 permute_h1(3)
             if i == G:
                 power(G - 2, 2, 2, nc.gpsimd)
                 difference(G - 2, 0, 2)
-            if i >= 1:
-                layer2(i - 1)
-            if 2 <= i < G:
-                power(i - 2, 2, 2, nc.vector)
-            if i >= 1:
-                clip_x(i - 1)
-            if i == G:
+                clip_x(G - 1)
                 natural_x(G - 2)
+            elif i >= 1:
+                layer2(i - 1)
+                if i >= 2:
+                    power(i - 2, 2, 2, nc.vector)
+                clip_x(i - 1)
             if 2 <= i < G:
                 difference(i - 2, 0, TL)
             if i < G:
@@ -444,6 +444,8 @@ def tile_qdtssolveronnx_pa_t_kernel(
                     sum_squares(i - 2, y, 0, TL, i - 2)
             if 1 <= i < G:
                 for tl in range(TL):
+                    if i == G - 1 and tl == 3:
+                        layer2(G - 1)
                     spectrum(i - 1, tl)
                     if tl == 1:
                         power(i - 1, 0, 2, nc.vector)

@@ -22,7 +22,7 @@ LAGS = 127
 G = 8
 TL = 4
 FLOPS = 2 * B * H * H + 2 * B * H * NOUT
-RELU_ON_VECTOR = (3, 7)
+RELU_ON_VECTOR = (7,)
 
 
 def tile_qdtssolveronnx_pa_t_kernel(
@@ -267,6 +267,7 @@ def tile_qdtssolveronnx_pa_t_kernel(
 
         nbv = nb[:].rearrange("p (g c t) -> p g t c", g=G, c=P, t=TL)
         xt = {}
+        xn = {}
         xct = {}
         sq = {}
         gt = {}
@@ -302,11 +303,13 @@ def tile_qdtssolveronnx_pa_t_kernel(
             px = psum.tile([P, TL, P], F32, tag="bank", name="px")
             for tl in range(TL):
                 nc.tensor.transpose(px[:, tl, :], xt[g][:, tl, :], ident_f[:])
-            xn = stage.tile([P, TL, P], F32, tag="xn", bufs=2, name="xn")
+            xn[g] = stage.tile([P, TL, P], F32, tag="xn", bufs=2, name="xn")
+            nc.scalar.copy(out=xn[g][:], in_=px[:])
+            nc.sync.dma_start(out=x_out[g], in_=xn[g][:])
+
+        def natural_xc(g, eng):
             xcn = stage.tile([P, TL, P], F32, tag="xcn", bufs=2, name="xcn")
-            nc.scalar.copy(out=xn[:], in_=px[:])
-            nc.gpsimd.tensor_scalar(out=xcn[:], in0=xn[:], scalar1=2.0, scalar2=-2.0, op0=ALU.min, op1=ALU.max)
-            nc.sync.dma_start(out=x_out[g], in_=xn[:])
+            eng.tensor_scalar(out=xcn[:], in0=xn[g][:], scalar1=2.0, scalar2=-2.0, op0=ALU.min, op1=ALU.max)
             nc.sync.dma_start(out=xc_out[g], in_=xcn[:])
 
         def spectrum(g, tl):
@@ -411,10 +414,11 @@ def tile_qdtssolveronnx_pa_t_kernel(
                 transpose_h1(2, (1, 1))
                 permute_h1(3)
             if i == G:
-                power(G - 2, 2, 2, nc.gpsimd)
                 difference(G - 2, 0, 2)
                 clip_x(G - 1)
+                power(G - 2, 2, 2, nc.vector)
                 natural_x(G - 2)
+                natural_xc(G - 2, nc.gpsimd)
             elif i >= 1:
                 layer2(i - 1)
                 if i >= 2:
@@ -422,6 +426,7 @@ def tile_qdtssolveronnx_pa_t_kernel(
                 clip_x(i - 1)
             if 2 <= i < G:
                 difference(i - 2, 0, TL)
+                natural_xc(i - 2, nc.vector)
             if i < G:
                 for ht in range(4):
                     layer1(i, ht)
@@ -471,6 +476,7 @@ def tile_qdtssolveronnx_pa_t_kernel(
                     if tl == 2:
                         sum_squares_v(G - 1, 0, 0, 2, G - 1)
                 natural_x(G - 1)
+                natural_xc(G - 1, nc.gpsimd)
                 sum_squares_v(G - 1, 0, 3, 1, G + 1)
                 sum_squares(G - 1, 1, 0, 2, G - 1)
                 for y in range(2):

@@ -172,18 +172,18 @@ def tile_qdtssolveronnx_pa_t_kernel(
             hg[g] = grouped
 
         def quantise_h1(g):
-            codes = stage.tile([P, 2 * 512], U32, tag="hq", bufs=2, name="hq", align_bytes=64)
-            scales = stage.tile([P, 2 * 512], U8, tag="hs", bufs=2, name="hs", align_bytes=64)
+            codes = stage.tile([P, 2 * 512], U32, tag="hq", bufs=2, name="hq", align_bytes=256)
+            scales = stage.tile([P, 2 * 512], U8, tag="hs", bufs=2, name="hs", align_bytes=256)
             nc.vector.quantize_mx(
                 out=codes[:].bitcast(FP8X4), scales=scales[:], in_=hg[g][:].rearrange("p g t c f -> p (g t c f)")
             )
             hq[g] = codes
             hs[g] = scales
 
-        wq = const.tile([P, 8, 2, P], U32, name="wq", align_bytes=64)
-        ws = const.tile([P, 8, 2, P], U8, name="ws", align_bytes=64)
-        woq = const.tile([P, 2, P], U32, name="woq", align_bytes=64)
-        wos = const.tile([P, 2, P], U8, name="wos", align_bytes=64)
+        wq = const.tile([P, 8, 2, P], U32, name="wq", align_bytes=256)
+        ws = const.tile([P, 8, 2, P], U8, name="ws", align_bytes=256)
+        woq = const.tile([P, 2, P], U32, name="woq", align_bytes=256)
+        wos = const.tile([P, 2, P], U8, name="wos", align_bytes=256)
 
         wp = {}
 
@@ -230,8 +230,8 @@ def tile_qdtssolveronnx_pa_t_kernel(
 
         def layer1(g, ht):
             if ht == 0:
-                h2q[g] = stage.tile([P, 2, 512], U32, tag="h2q", bufs=2, name="h2q", align_bytes=64)
-                h2s[g] = stage.tile([P, 2, 512], U8, tag="h2s", bufs=2, name="h2s", align_bytes=64)
+                h2q[g] = stage.tile([P, 2, 512], U32, tag="h2q", bufs=2, name="h2q", align_bytes=256)
+                h2s[g] = stage.tile([P, 2, 512], U8, tag="h2s", bufs=2, name="h2s", align_bytes=256)
             if ht % 4 == 0:
                 planes[g] = stage.tile([P, 4, 512], BF16, tag="h2p", bufs=3, name="h2p")
             pm = psum.tile([P, 512], F32, tag="bank", name="pm")

from contextlib import ExitStack
import math

import concourse.masks as masks
import concourse.mybir as mybir

F32 = mybir.dt.float32
BF16 = mybir.dt.bfloat16
I32 = mybir.dt.int32
U32 = mybir.dt.uint32
U8 = mybir.dt.uint8
FP8X4 = mybir.dt.float8_e4m3fn_x4
ALU = mybir.AluOpType
ACT = mybir.ActivationFunctionType
AX = mybir.AxisListType

P = 128
B = 4096
H = 1024
NOUT = 128
LAGS = 127
G = 8
TL = 4
FLOPS = 2 * B * H * H + 2 * B * H * NOUT
RELU_ON_VECTOR = (7,)


def tile_qdtssolveronnx_pa_t_kernel(
    tc, h1, w_hid2, b_hid2, w_out, b_out, norm_root, T, out_0, out_1, out_2, out_3
):
    nc = tc.nc
    with ExitStack() as ctx:
        ctx.enter_context(tc.manual_schedule())
        const = ctx.enter_context(tc.tile_pool(name="const", bufs=1))
        stage = ctx.enter_context(tc.tile_pool(name="stage", bufs=2))
        psum = ctx.enter_context(tc.psum_pool(name="psum", bufs=8))

        h1v = h1.rearrange("(g p t) k -> g p t k", g=G, p=P, t=TL)
        wv = w_hid2.rearrange("(g p j) k -> g p j k", g=2, p=P, j=4)
        tv = T.rearrange("(g p t) k -> p g (t k)", g=G, p=P, t=TL)
        x_out = out_0.rearrange("(g p t) j -> g p t j", g=G, p=P, t=TL)
        xc_out = out_2.rearrange("(g p t) j -> g p t j", g=G, p=P, t=TL)

        ones = const.tile([P, P], F32, name="ones")
        nc.vector.memset(ones[:], 1.0)
        warm = psum.tile([P, 512], F32, tag="bank", name="warm")
        for n in range(4):
            nc.tensor.matmul(warm[:, 0:P], lhsT=ones[:], rhs=ones[:], start=True, stop=True)

        hsb = {}

        def load_h1(g):
            t = stage.tile([P, TL, H], BF16, tag="hsb", bufs=3, name="hsb")
            nc.sync.dma_start(out=t[:], in_=h1v[g])
            hsb[g] = t

        tsb = const.tile([P, G, 512], BF16, name="tsb")
        nc.vector.memset(tsb[:, :, 496:512], 0.0)
        for g0, g1 in ((0, 1), (1, 4), (4, G)):
            nc.sync.dma_start(out=tsb[:, g0:g1, 0 : TL * LAGS], in_=tv[:, g0:g1, :])
        load_h1(0)
        wsb = []
        for g2 in range(2):
            wt = stage.tile([P, 4, H], BF16, tag="sq", bufs=2, name="wsb")
            wsb.append(wt)
            for h in range(2):
                nc.sync.dma_start(out=wt[:, 2 * h : 2 * h + 2, :], in_=wv[g2][:, 2 * h : 2 * h + 2, :])
        wosb = const.tile([P, H], BF16, name="wosb")
        nc.scalar.dma_start(out=wosb[:], in_=w_out)
        bh_b = const.tile([P, 2, 4], BF16, name="bh_b")
        bo_b = const.tile([P, 1], BF16, name="bo_b")
        with nc.allow_non_contiguous_dma(reason="two small bias vectors, one or four elements a partition"):
            nc.scalar.dma_start(out=bh_b[:], in_=b_hid2.rearrange("(g p j) -> p g j", g=2, p=P, j=4))
            nc.scalar.dma_start(out=bo_b[:], in_=b_out.rearrange("(p o) -> p o", o=1))
        load_h1(1)
        load_h1(2)
        nb = const.tile([P, B], BF16, name="nb")
        nc.sync.dma_start(out=nb[:], in_=norm_root.rearrange("b o -> (b o)").partition_broadcast(P))
        load_h1(3)

        odd_f = const.tile([P, P], F32, name="odd_f")
        nc.gpsimd.iota(odd_f[:], pattern=[[2, P]], base=1, channel_multiplier=0, allow_small_or_imprecise_dtypes=True)
        row_f = const.tile([P, 1], F32, name="row_f")
        nc.gpsimd.iota(row_f[:], pattern=[[1, 1]], base=0, channel_multiplier=1, allow_small_or_imprecise_dtypes=True)
        ident_b = const.tile([P, P], BF16, name="ident_b")
        masks.make_identity(nc, ident_b[:])
        ident_f = const.tile([P, P], F32, name="ident_f")
        masks.make_identity(nc, ident_f[:])

        lag_f = const.tile([P, 1], F32, name="lag_f")
        nc.vector.tensor_scalar(out=lag_f[:], in0=row_f[:], scalar1=-1.0, scalar2=float(LAGS), op0=ALU.mult, op1=ALU.add)
        lag_w = const.tile([P, 1], F32, name="lag_w")
        nc.vector.tensor_scalar(out=lag_w[:], in0=row_f[:], scalar1=float(LAGS), scalar2=2.0, op0=ALU.is_lt, op1=ALU.mult)
        cnt_i = const.tile([P, 3, P], I32, name="cnt_i")
        nc.vector.tensor_scalar(out=cnt_i[:, 2, :], in0=odd_f[:], scalar1=lag_f[:, 0:1], scalar2=384.0, op0=ALU.mult, op1=ALU.add)
        nc.vector.tensor_scalar(out=cnt_i[:, 0, :], in0=odd_f[:], scalar1=row_f[:, 0:1], scalar2=384.0, op0=ALU.mult, op1=ALU.add)
        nc.vector.tensor_scalar(out=cnt_i[:, 1, :], in0=odd_f[:], scalar1=row_f[:, 0:1], scalar2=256.0, op0=ALU.mult, op1=ALU.add)
        cnt_m = const.tile([P, 3, P], I32, name="cnt_m")
        nc.vector.tensor_single_scalar(out=cnt_m[:], in_=cnt_i[:], scalar=511, op=ALU.bitwise_and)
        ang = const.tile([P, 3, P], F32, name="ang")
        nc.vector.tensor_scalar(out=ang[:], in0=cnt_m[:], scalar1=-256.0, scalar2=math.pi / 256.0, op0=ALU.add, op1=ALU.mult)
        trig = const.tile([P, 3, P], F32, name="trig")
        nc.scalar.activation(out=trig[:], in_=ang[:], func=ACT.Sin)
        ftab = trig[:, 0:2, :].rearrange("p a m -> p (a m)")
        cterm = const.tile([P, 3, P], BF16, name="cterm")
        crest = const.tile([P, P], F32, name="crest")
        nc.vector.tensor_scalar(out=cterm[:, 0, :], in0=trig[:, 2, :], scalar1=lag_w[:, 0:1], scalar2=None, op0=ALU.mult)
        nc.vector.scalar_tensor_tensor(
            out=crest[:], in0=trig[:, 2, :], scalar=lag_w[:, 0:1], in1=cterm[:, 0, :], op0=ALU.mult, op1=ALU.subtract
        )
        nc.vector.tensor_copy(out=cterm[:, 1, :], in_=crest[:])
        nc.vector.tensor_tensor(out=cterm[:, 2, :], in0=crest[:], in1=cterm[:, 1, :], op=ALU.subtract)

        bh = const.tile([P, 8], F32, name="bh")
        bo = const.tile([P, 1], F32, name="bo")

        count = float(B * LAGS)
        r0acc = const.tile([P, 2, G * TL], F32, name="r0acc")
        s1 = const.tile([P, G + 4, 2], F32, name="s1")
        minus = const.tile([P, P], F32, name="minus")
        nc.gpsimd.memset(minus[:], -1.0)

        def copy_out(which, out, in_):
            if which == 0:
                nc.vector.tensor_copy(out=out, in_=in_)
            else:
                nc.scalar.copy(out=out, in_=in_)

        def word_transposes(words):
            pt = psum.tile([P, 2, 2, P], F32, tag="bank", name="pt")
            for gk in range(2):
                for u in range(2):
                    nc.tensor.transpose(pt[:, gk, u, :], words(gk, u), ident_f[:])
            return pt

        tta = const.tile([P, G, TL, P], BF16, name="tta")
        usb = const.tile([P, G, TL * P], F32, name="usb")

        def transpose_t(g):
            ptt = psum.tile([P, TL, P], BF16, tag="bank", name="ptt")
            for tl in range(TL):
                nc.tensor.transpose(ptt[:, tl, :], tsb[:, g, LAGS * tl : LAGS * tl + P], ident_b[:])
            copy_out(g % 2, tta[:, g], ptt[:])

        def transform_t(g, which):
            pu = psum.tile([P, TL, P], F32, tag="bank", name="pu")
            for tl in range(TL):
                for term in range(3):
                    nc.tensor.matmul(
                        pu[:, tl, :], lhsT=tta[:, g, tl, :], rhs=cterm[:, term, :], start=(term == 0), stop=(term == 2)
                    )
            copy_out(which, usb[:, g, :], pu[:].rearrange("p t m -> p (t m)"))

        hg = {}
        hq = {}
        hs = {}

        hp = {}

        def permute_h1(g):
            hp[g] = stage.tile([P, TL * 2, 2, P], F32, tag="hp", bufs=2, name="hp")
            nc.vector.tensor_copy(
                out=hp[g][:], in_=hsb[g][:].bitcast(F32).rearrange("p t (g c u) -> p (t g) u c", g=2, u=2)
            )

        def transpose_h1(g, engines):
            grouped = stage.tile([P, 2, TL, P, 4], BF16, tag="hg", bufs=2, name="hg", align_bytes=64)
            gw = grouped[:].bitcast(F32)
            for tl in range(TL):
                pt = word_transposes(lambda gk, u: hp[g][:, 2 * tl + gk, u, :])
                copy_out(engines[tl % 2], gw[:, :, tl, :, :], pt[:].rearrange("p g u c -> p g c u"))
            hg[g] = grouped

        def quantise_h1(g):
            codes = stage.tile([P, 2 * 512], U32, tag="hq", bufs=2, name="hq", align_bytes=256)
            scales = stage.tile([P, 2 * 512], U8, tag="hs", bufs=2, name="hs", align_bytes=256)
            nc.vector.quantize_mx(
                out=codes[:].bitcast(FP8X4), scales=scales[:], in_=hg[g][:].rearrange("p g t c f -> p (g t c f)")
            )
            hq[g] = codes
            hs[g] = scales

        wq = const.tile([P, 8, 2, P], U32, name="wq", align_bytes=256)
        ws = const.tile([P, 8, 2, P], U8, name="ws", align_bytes=256)
        woq = const.tile([P, 2, P], U32, name="woq", align_bytes=256)
        wos = const.tile([P, 2, P], U8, name="wos", align_bytes=256)

        wp = {}

        def permute_w(pair):
            wp[pair] = stage.tile([P, 4, 2, P], F32, tag="wp", bufs=3, name="wp")
            rows = 2 * (pair % 2)
            nc.vector.tensor_copy(
                out=wp[pair][:],
                in_=wsb[pair // 2][:, rows : rows + 2, :].bitcast(F32).rearrange("p t (g c u) -> p (t g) u c", g=2, u=2),
            )

        def prepare_w(pair):
            grouped = stage.tile([P, 2, 2, P, 4], BF16, tag="wg", bufs=2, name="wg", align_bytes=64)
            gw = grouped[:].bitcast(F32)
            for h in range(2):
                pt = word_transposes(lambda gk, u: wp[pair][:, 2 * h + gk, u, :])
                copy_out(1, gw[:, h], pt[:].rearrange("p g u c -> p g c u"))
            return grouped

        def quantise_w(pair, grouped):
            nc.vector.quantize_mx(
                out=wq[:, 2 * pair : 2 * pair + 2].rearrange("p h g c -> p (h g c)").bitcast(FP8X4),
                scales=ws[:, 2 * pair : 2 * pair + 2].rearrange("p h g c -> p (h g c)"),
                in_=grouped[:].rearrange("p h g c f -> p (h g c f)"),
            )

        def prepare_w_out():
            wow = wosb[:].bitcast(F32).rearrange("o (g p u) -> o g u p", g=2, p=P, u=2)
            grouped = stage.tile([P, 2, P, 4], BF16, tag="wog", bufs=1, name="wog", align_bytes=64)
            pt = word_transposes(lambda g2, u: wow[:, g2, u, :])
            copy_out(1, grouped[:].bitcast(F32), pt[:].rearrange("p g u c -> p g c u"))
            return grouped

        def quantise_w_out(grouped):
            nc.vector.quantize_mx(
                out=woq[:].rearrange("p g c -> p (g c)").bitcast(FP8X4),
                scales=wos[:].rearrange("p g c -> p (g c)"),
                in_=grouped[:].rearrange("p g c f -> p (g c f)"),
            )

        h2q = {}
        h2s = {}
        planes = {}

        def layer1(g, ht):
            if ht == 0:
                h2q[g] = stage.tile([P, 2, 512], U32, tag="h2q", bufs=2, name="h2q", align_bytes=256)
                h2s[g] = stage.tile([P, 2, 512], U8, tag="h2s", bufs=2, name="h2s", align_bytes=256)
            if ht % 4 == 0:
                planes[g] = stage.tile([P, 4, 512], BF16, tag="h2p", bufs=3, name="h2p")
            pm = psum.tile([P, 512], F32, tag="bank", name="pm")
            for gk in range(2):
                nc.tensor.matmul_mx(
                    out=pm[:],
                    lhsT=wq[:, ht, gk, :].bitcast(FP8X4),
                    lhsT_scale=ws[:, ht, gk, :],
                    rhs=hq[g][:, 512 * gk : 512 * gk + 512].bitcast(FP8X4),
                    rhs_scale=hs[g][:, 512 * gk : 512 * gk + 512],
                    start=(gk == 0),
                    stop=(gk == 1),
                )
            if ht in RELU_ON_VECTOR:
                nc.vector.tensor_scalar(
                    out=planes[g][:, ht % 4, :], in0=pm[:], scalar1=bh[:, ht : ht + 1], scalar2=0.0, op0=ALU.add, op1=ALU.max
                )
            else:
                nc.scalar.activation(out=planes[g][:, ht % 4, :], in_=pm[:], func=ACT.Relu, bias=bh[:, ht : ht + 1])

        def regroup_h2(g):
            grouped = stage.tile([P, 512, 4], BF16, tag="h2g", bufs=2, name="h2g", align_bytes=64)
            nc.vector.tensor_copy(
                out=grouped[:].rearrange("p (c i) t -> p c t i", i=4),
                in_=planes[g][:].rearrange("p t (c i) -> p c t i", i=4),
            )
            return grouped

        def quantise_h2(g, g2, grouped):
            nc.vector.quantize_mx(
                out=h2q[g][:, g2, :].bitcast(FP8X4), scales=h2s[g][:, g2, :], in_=grouped[:].rearrange("p c t -> p (c t)")
            )

        nbv = nb[:].rearrange("p (g c t) -> p g t c", g=G, c=P, t=TL)
        xt = {}
        xn = {}
        xct = {}
        sq = {}
        gt = {}
        dt_ = {}

        def layer2(g):
            pm = psum.tile([P, 512], F32, tag="bank", name="pm2")
            for g2 in range(2):
                nc.tensor.matmul_mx(
                    out=pm[:],
                    lhsT=woq[:, g2, :].bitcast(FP8X4),
                    lhsT_scale=wos[:, g2, :],
                    rhs=h2q[g][:, g2, :].bitcast(FP8X4),
                    rhs_scale=h2s[g][:, g2, :],
                    start=(g2 == 0),
                    stop=(g2 == 1),
                )
            xt[g] = stage.tile([P, TL, P], F32, tag="xt", bufs=2, name="xt")
            nc.vector.scalar_tensor_tensor(
                out=xt[g][:],
                in0=pm[:].rearrange("p (t c) -> p t c", t=TL),
                scalar=bo[:, 0:1],
                in1=nbv[:, g],
                op0=ALU.add,
                op1=ALU.mult,
            )

        def clip_x(g):
            xct[g] = stage.tile([P, TL, P], F32, tag="xct", bufs=2, name="xct")
            nc.vector.tensor_scalar(out=xct[g][:], in0=xt[g][:], scalar1=2.0, scalar2=-2.0, op0=ALU.min, op1=ALU.max)

        def natural_x(g):
            px = psum.tile([P, TL, P], F32, tag="bank", name="px")
            for tl in range(TL):
                nc.tensor.transpose(px[:, tl, :], xt[g][:, tl, :], ident_f[:])
            xn[g] = stage.tile([P, TL, P], F32, tag="xn", bufs=2, name="xn")
            nc.scalar.copy(out=xn[g][:], in_=px[:])
            nc.sync.dma_start(out=x_out[g], in_=xn[g][:])

        def natural_xc(g, eng):
            xcn = stage.tile([P, TL, P], F32, tag="xcn", bufs=2, name="xcn")
            eng.tensor_scalar(out=xcn[:], in0=xn[g][:], scalar1=2.0, scalar2=-2.0, op0=ALU.min, op1=ALU.max)
            nc.sync.dma_start(out=xc_out[g], in_=xcn[:])

        def spectrum(g, tl):
            if tl == 0:
                sq[g] = stage.tile([P, TL, 2, 2 * P], F32, tag="sq", bufs=2, name="sq")
                gt[g] = stage.tile([P, 2, TL, P], F32, tag="gt", bufs=2, name="gt")
            pd = psum.tile([P, 2, 2 * P], F32, tag="bank", name="pd")
            nc.tensor.matmul(pd[:, 0, :], lhsT=xt[g][:, tl, :], rhs=ftab, start=True, stop=True)
            nc.tensor.matmul(pd[:, 1, :], lhsT=xct[g][:, tl, :], rhs=ftab, start=True, stop=True)
            for y in range(2):
                nc.scalar.activation(
                    out=sq[g][:, tl, y, :],
                    in_=pd[:, y, :],
                    func=ACT.Square,
                    accum_out=r0acc[:, y, TL * g + tl : TL * g + tl + 1],
                )

        def power(g, t0, nt, eng):
            eng.tensor_tensor(
                out=gt[g][:, :, t0 : t0 + nt, :],
                in0=sq[g][:, t0 : t0 + nt, :, 0:P].rearrange("p t y m -> p y t m"),
                in1=sq[g][:, t0 : t0 + nt, :, P : 2 * P].rearrange("p t y m -> p y t m"),
                op=ALU.add,
            )

        def difference(g, t0, nt):
            if t0 == 0:
                dt_[g] = stage.tile([P, 2, TL, P], F32, tag="dt", bufs=2, name="dt")
            nc.vector.tensor_tensor(
                out=dt_[g][:, :, t0 : t0 + nt, :].rearrange("p y t m -> p y (t m)"),
                in0=gt[g][:, :, t0 : t0 + nt, :].rearrange("p y t m -> p y (t m)"),
                in1=usb[:, g, P * t0 : P * (t0 + nt)].unsqueeze(1).to_broadcast([P, 2, P * nt]),
                op=ALU.subtract,
            )

        def sum_squares(g, y, t0, nt, col):
            junk = stage.tile([P, TL * P], F32, tag="junk", bufs=1, name="junk")
            nc.scalar.activation(
                out=junk[:, 0 : P * nt],
                in_=dt_[g][:, y, t0 : t0 + nt, :].rearrange("p t m -> p (t m)"),
                func=ACT.Square,
                scale=(1.0 / (256.0 * count)) ** 0.5,
                accum_out=s1[:, col, y : y + 1],
            )

        def sum_squares_v(g, y, t0, nt, col):
            junk = stage.tile([P, TL * P], F32, tag="junkv", bufs=1, name="junkv")
            d = dt_[g][:, y, t0 : t0 + nt, :].rearrange("p t m -> p (t m)")
            nc.vector.scalar_tensor_tensor(
                out=junk[:, 0 : P * nt],
                in0=d,
                scalar=1.0 / (256.0 * count),
                in1=d,
                op0=ALU.mult,
                op1=ALU.mult,
                accum_out=s1[:, col, y : y + 1],
            )

        def sum_r0(t0, t1, col):
            for y in range(2):
                junk = stage.tile([P, G * TL], F32, tag="junkr", bufs=1, name="junkr")
                nc.scalar.activation(
                    out=junk[:, 0 : t1 - t0],
                    in_=r0acc[:, y, t0:t1],
                    func=ACT.Square,
                    scale=(1.0 / (2.0 * 128.0 * 128.0 * count)) ** 0.5,
                    accum_out=s1[:, col, y : y + 1],
                )

        for g in range(G):
            transpose_t(g)
        transform_t(0, 1)
        transform_t(1, 1)
        permute_h1(0)
        permute_w(0)
        transpose_h1(0, (0, 1))
        transform_t(2, 1)
        permute_w(1)
        wg0 = prepare_w(0)
        transform_t(3, 1)
        quantise_h1(0)
        nc.vector.tensor_copy(out=bh[:], in_=bh_b[:].rearrange("p g j -> p (g j)"))
        nc.vector.tensor_copy(out=bo[:], in_=bo_b[:])
        permute_w(2)
        wg1 = prepare_w(1)
        quantise_w(0, wg0)
        transform_t(4, 1)
        permute_w(3)
        wg2 = prepare_w(2)
        quantise_w(1, wg1)
        permute_h1(1)
        wg3 = prepare_w(3)
        quantise_w(2, wg2)
        wog = prepare_w_out()
        quantise_w(3, wg3)
        quantise_w_out(wog)

        for i in range(G + 1):
            if i + 4 < G:
                load_h1(i + 4)
            if i == 1:
                transpose_h1(2, (1, 1))
                permute_h1(3)
            if i == G:
                difference(G - 2, 0, 2)
                clip_x(G - 1)
                power(G - 2, 2, 2, nc.vector)
                natural_x(G - 2)
                natural_xc(G - 2, nc.gpsimd)
            elif i >= 1:
                layer2(i - 1)
                if i >= 2:
                    power(i - 2, 2, 2, nc.vector)
                clip_x(i - 1)
            if 2 <= i < G:
                difference(i - 2, 0, TL)
                natural_xc(i - 2, nc.vector)
            if i < G:
                for ht in range(4):
                    layer1(i, ht)
                ga = regroup_h2(i)
                if i == 0:
                    transpose_h1(1, (1, 1))
                    permute_h1(2)
                for ht in range(4, 8):
                    layer1(i, ht)
                gb = regroup_h2(i)
                quantise_h2(i, 0, ga)
                quantise_h2(i, 1, gb)
                if i + 1 < G:
                    quantise_h1(i + 1)
            if i == 0:
                for g in range(5, G):
                    transform_t(g, 1)
            if 2 <= i < G:
                for y in range(2):
                    sum_squares(i - 2, y, 0, TL, i - 2)
            if 1 <= i < G:
                for tl in range(TL):
                    if i == G - 1 and tl == 3:
                        layer2(G - 1)
                    spectrum(i - 1, tl)
                    if tl == 1:
                        power(i - 1, 0, 2, nc.vector)
                    if tl == 1:
                        if i + 2 < G:
                            transpose_h1(i + 2, (1, 1))
                        if i + 3 < G:
                            permute_h1(i + 3)
                        if i < G - 1:
                            natural_x(i - 1)
            if i == G:
                difference(G - 2, 2, 2)
                sum_r0(0, TL * (G - 1), G + 2)
                sum_squares_v(G - 2, 0, 0, TL, G - 2)
                for tl in range(TL):
                    spectrum(G - 1, tl)
                    if tl == 1:
                        sum_squares(G - 2, 1, 0, TL, G - 2)
                    if tl >= 1:
                        t0, nt = (0, 2) if tl == 1 else (tl, 1)
                        power(G - 1, t0, nt, nc.vector)
                        difference(G - 1, t0, nt)
                    if tl == 2:
                        sum_squares_v(G - 1, 0, 0, 2, G - 1)
                natural_x(G - 1)
                natural_xc(G - 1, nc.gpsimd)
                sum_squares_v(G - 1, 0, 3, 1, G + 1)
                sum_squares(G - 1, 1, 0, 2, G - 1)
                for y in range(2):
                    sum_squares(G - 1, y, 2, 1, G)
                sum_r0(TL * (G - 1), TL * G, G + 3)
                sum_squares(G - 1, 1, 3, 1, G + 1)

        pf = psum.tile([P, G + 4, 2], F32, tag="bank", name="pf")
        nc.tensor.matmul(
            pf[:, G + 2 :, :].rearrange("p c y -> p (c y)"),
            lhsT=minus[:],
            rhs=s1[:, G + 2 :, :].rearrange("p c y -> p (c y)"),
            start=True,
            stop=True,
        )
        nc.tensor.matmul(
            pf[:, 0 : G + 2, :].rearrange("p c y -> p (c y)"),
            lhsT=ones[:],
            rhs=s1[:, 0 : G + 2, :].rearrange("p c y -> p (c y)"),
            start=True,
            stop=True,
        )
        res = const.tile([P, 2], F32, name="res")
        nc.vector.tensor_reduce(out=res[:], in_=pf[:].rearrange("p c y -> p y c"), axis=AX.X, op=ALU.add)
        nc.sync.dma_start(out=out_1.rearrange("(a b) -> a b", a=1), in_=res[0:1, 0:1])
        nc.scalar.dma_start(out=out_3.rearrange("(a b) -> a b", a=1), in_=res[0:1, 1:2])
